import numpy as np
import ml_dtypes


def mxq(x, axis, fmt="e4m3"):
    dtype, down = {"e4m3": (ml_dtypes.float8_e4m3fn, 7), "e5m2": (ml_dtypes.float8_e5m2, 14)}[fmt]
    v = np.moveaxis(np.asarray(x, np.float32).astype(ml_dtypes.bfloat16).astype(np.float64), axis, -1)
    blocks = v.reshape(v.shape[:-1] + (-1, 32))
    amax = np.abs(blocks).max(-1, keepdims=True)
    byte = np.maximum(np.where(amax > 0, np.frexp(amax)[1] - 1 + 127, 0) - down, 1)
    scale = np.exp2(byte - 127.0)
    codes = (blocks / scale).astype(np.float32).astype(dtype).astype(np.float64)
    return np.moveaxis((codes * scale).reshape(v.shape), -1, axis)


WIDE = False


def mx_kscale(k):
    if not WIDE:
        return np.ones(k)
    levels = np.array([10, -10, 5, -5, 0])
    a = np.random.permutation(np.resize(levels, k // 512 * 4)).reshape(k // 512, 4)
    idx = np.arange(k)
    return np.exp2(a[idx // 512, idx % 128 // 32])


BF16 = ml_dtypes.bfloat16


def bf(x):
    return np.asarray(x, np.float32).astype(BF16)


def f64(x):
    return np.asarray(x).astype(np.float64)


E2M1 = np.array([0.0, 0.5, 1.0, 1.5, 2.0, 3.0, 4.0, 6.0, -0.0, -0.5, -1.0, -1.5, -2.0, -3.0, -4.0, -6.0])


def pack_weight(w, fmt):
    k, n = w.shape
    w = f64(bf(w)).reshape(k // 32, 32, n)
    amax = np.abs(w).max(1)
    if fmt == "e4m3":
        byte = np.frexp(amax)[1] - 1 + 127 - 7
    else:
        mant, ex = np.frexp(amax / 6.0)
        byte = np.where(mant > 0.5, ex, ex - 1) + 127
    byte = np.clip(np.where(amax > 0, byte, 1), 1, 254)
    scaled = (w * np.exp2(127.0 - byte)[:, None, :]).reshape(k, n).astype(np.float32)
    by_word = np.ascontiguousarray(scaled.reshape(k // 512, 128, 4, n).transpose(0, 1, 3, 2))
    if fmt == "e4m3":
        words = by_word.astype(ml_dtypes.float8_e4m3fn).view(np.uint8)
    else:
        c = by_word.astype(ml_dtypes.float4_e2m1fn).view(np.uint8) & 0xF
        words = c[..., 0::2] | (c[..., 1::2] << 4)
    return np.ascontiguousarray(words), np.ascontiguousarray(byte.astype(np.uint8).reshape(k // 512, 16, n))


def unpack_weight(words, scales, fmt):
    g, p, n, _ = words.shape
    if fmt == "e4m3":
        vals = np.ascontiguousarray(words).view(ml_dtypes.float8_e4m3fn).astype(np.float64)
    else:
        nib = np.empty((g, p, n, 4), np.uint8)
        nib[..., 0::2] = words & 0xF
        nib[..., 1::2] = words >> 4
        vals = E2M1[nib]
    vals = vals * np.repeat(np.exp2(scales.astype(np.float64) - 127.0), 8, axis=1)[..., None]
    return vals.transpose(0, 1, 3, 2).reshape(g * 512, n)


N, C, D, H, W = 2, 1, 4096, 8, 8
EPS = 1e-5


def setup_inputs():
    t = np.minimum(mx_kscale(D), 1.0) ** 2
    sig0 = 0.01 * (0.5 + np.random.random_sample((C, D)))
    sig = sig0 * t
    r = np.exp2(np.round(np.log2((sig / np.sqrt(sig**2 + EPS)) / (sig0 / np.sqrt(sig0**2 + EPS)))))
    mu = np.random.standard_normal((C, D))
    z = np.random.standard_normal((N, C, D, H, W))
    x = ((z + mu[None, :, :, None, None]) * sig[None, :, :, None, None]).reshape(N, C * D, H, W)
    weight = (np.eye(D)[None] + np.random.standard_normal((C, D, D)) / np.sqrt(D)) / r[:, None, :]
    cat = np.ascontiguousarray(np.swapaxes(weight, 1, 2)).reshape(-1, D)
    words, scales = pack_weight(cat, "e4m3")
    return {"x": bf(x), "weight_words": words, "weight_scales": scales, "bias": bf(np.random.standard_normal(C * D) * 0.3)}


def reference(x, weight_words, weight_scales, bias):
    x, bias = f64(x), f64(bias)
    n, cd, h, w = x.shape
    c = C
    d = cd // c
    mean = np.mean(x, axis=(0, 2, 3), keepdims=True)
    var = np.mean(np.square(x - mean), axis=(0, 2, 3), keepdims=True)
    xn = (x - mean) / np.sqrt(var + EPS)
    xg = xn.reshape(n, c, d, h * w)
    out = unpack_weight(weight_words, weight_scales, "e4m3").reshape(C, D, D).swapaxes(1, 2)[None] @ mxq(xg, 2, "e4m3")
    return out.reshape(n, cd, h, w) + bias[None, :, None, None]

@@ -1,0 +1,140 @@
+from contextlib import ExitStack
+
+import concourse.mybir as mybir
+from concourse.masks import make_identity
+
+FP8X4 = mybir.dt.float8_e4m3fn_x4
+BF16 = mybir.dt.bfloat16
+F32 = mybir.dt.float32
+I32 = mybir.dt.int32
+U32 = mybir.dt.uint32
+U8 = mybir.dt.uint8
+ALU = mybir.AluOpType
+
+P = 128
+PACK = 4
+K_PASS = P * PACK
+BATCH, CHANNELS, HW = 2, 4096, 64
+PIXELS = BATCH * HW
+PASSES = CHANNELS // K_PASS
+BANK_COLS = 512
+BANKS = CHANNELS // BANK_COLS
+RUN = BANK_COLS // P
+PLANES_PER_TILE = 4
+QUADRANTS = 4
+EPS = 1e-5
+BN_STATS_DIM = 6
+FLOPS = 2 * CHANNELS * CHANNELS * PIXELS
+
+
+def tile_caps_bn_w_e_kernel(tc, x, weight_words, weight_scales, bias, out):
+    nc = tc.nc
+    with ExitStack() as stack:
+        keep = stack.enter_context(tc.tile_pool(name="keep", bufs=1))
+        work = stack.enter_context(tc.tile_pool(name="work", bufs=3))
+        psum = stack.enter_context(tc.psum_pool(name="psum", bufs=BANKS))
+
+        x_sb = keep.tile([P, BATCH, PASSES, PACK, HW], BF16)
+        nc.sync.dma_start(
+            out=x_sb[:].rearrange("p n g t f -> p n g (t f)"),
+            in_=x.rearrange("n (g p t) h w -> p n g (t h w)", p=P, t=PACK),
+        )
+
+        planes = [
+            keep.tile([P, CHANNELS], U8, align_bytes=64, name="planes%d" % a) for a in range(PASSES // PLANES_PER_TILE)
+        ]
+        scales_i32 = weight_scales.bitcast(I32)
+        for plane_tile in planes:
+            nc.vector.memset(plane_tile[:].bitcast(I32), 0)
+        for a, plane_tile in enumerate(planes):
+            for quad in range(QUADRANTS):
+                nc.sync.dma_start(
+                    out=plane_tile[32 * quad : 32 * quad + 4 * PLANES_PER_TILE, :].bitcast(I32),
+                    in_=scales_i32[PLANES_PER_TILE * a : PLANES_PER_TILE * (a + 1), 4 * quad : 4 * quad + 4, :],
+                )
+
+        w_sb = keep.tile([P, PASSES, CHANNELS], U32, align_bytes=64)
+        w_dram = weight_words.rearrange("g p n t -> p g (n t)").bitcast(I32)
+        for g in range(PASSES - 1):
+            nc.sync.dma_start(out=w_sb[:, g, :].bitcast(I32), in_=w_dram[:, g, :])
+        for b in range(BANKS):
+            cols = slice(b * BANK_COLS, (b + 1) * BANK_COLS)
+            nc.sync.dma_start(out=w_sb[:, PASSES - 1, cols].bitcast(I32), in_=w_dram[:, PASSES - 1, cols])
+
+        bias_bf = keep.tile([P, BANKS, RUN], BF16)
+        nc.scalar.dma_start(out=bias_bf[:], in_=bias.rearrange("(b c j) -> c b j", c=P, j=RUN))
+        bias_f32 = keep.tile([P, BANKS, RUN], F32)
+        nc.vector.tensor_copy(out=bias_f32[:], in_=bias_bf[:])
+
+        ident = keep.tile([P, P], F32)
+        make_identity(nc, ident[:])
+
+        stats = keep.tile([P, PASSES, PACK, BN_STATS_DIM], F32)
+        mean_var = keep.tile([P, PASSES, PACK, 2], F32)
+        for g in range(PASSES):
+            for t in range(PACK):
+                nc.vector.bn_stats(out=stats[:, g, t, :], in_=x_sb[:, :, g, t, :])
+        for g in range(PASSES):
+            for t in range(PACK):
+                nc.vector.bn_aggr(out=mean_var[:, g, t, :], in_=stats[:, g, t, :])
+        var_eps = keep.tile([P, PASSES, PACK], F32)
+        nc.vector.tensor_scalar_add(out=var_eps[:], in0=mean_var[:, :, :, 1], scalar1=EPS)
+        std = keep.tile([P, PASSES, PACK], F32)
+        nc.scalar.sqrt(out=std[:], in_=var_eps[:])
+        rstd = keep.tile([P, PASSES, PACK], F32)
+        nc.vector.reciprocal(out=rstd[:], in_=std[:])
+
+        grouped = keep.tile([P, PASSES, PIXELS, PACK], BF16, align_bytes=64)
+        xq_words = keep.tile([P, PASSES, PIXELS], U32, align_bytes=64)
+        xq_scales = keep.tile([P, PASSES, PIXELS], U8, align_bytes=64)
+        for g in range(PASSES):
+            for t in range(PACK):
+                nc.vector.tensor_scalar(
+                    out=grouped[:, g, :, t].rearrange("p (n f) -> p n f", n=BATCH),
+                    in0=x_sb[:, :, g, t, :],
+                    scalar1=mean_var[:, g, t, 0:1],
+                    scalar2=rstd[:, g, t : t + 1],
+                    op0=ALU.subtract,
+                    op1=ALU.mult,
+                )
+            nc.vector.quantize_mx(
+                out=xq_words[:, g, :].bitcast(FP8X4),
+                scales=xq_scales[:, g, :],
+                in_=grouped[:, g, :, :].rearrange("p c t -> p (c t)"),
+            )
+
+        acc = [psum.tile([P, BANK_COLS], F32, name="acc%d" % b, tag="bank") for b in range(BANKS)]
+
+        def mx_pass(g, b):
+            cols = slice(b * BANK_COLS, (b + 1) * BANK_COLS)
+            first_row = 4 * (g % PLANES_PER_TILE)
+            nc.tensor.matmul_mx(
+                out=acc[b][:],
+                lhsT=xq_words[:, g, :].bitcast(FP8X4),
+                lhsT_scale=xq_scales[:, g, :],
+                rhs=w_sb[:, g, cols].bitcast(FP8X4),
+                rhs_scale=planes[g // PLANES_PER_TILE][first_row:P, cols],
+                start=(g == 0),
+                stop=(g == PASSES - 1),
+            )
+
+        for g in range(PASSES - 1):
+            for b in range(BANKS):
+                mx_pass(g, b)
+
+        out_by_bank = out.rearrange("n (b c j) h w -> b c n (j h w)", c=P, j=RUN)
+        for b in range(BANKS):
+            mx_pass(PASSES - 1, b)
+            sorted_cols = work.tile([P, RUN, P], F32)
+            nc.scalar.copy(out=sorted_cols[:], in_=acc[b][:].rearrange("p (c j) -> p j c", j=RUN))
+            turned = psum.tile([P, RUN, PIXELS], F32, tag="bank")
+            for j in range(RUN):
+                nc.tensor.transpose(turned[:, j, :], sorted_cols[:, j, :], ident[:])
+            result = work.tile([P, BATCH, RUN, HW], F32)
+            nc.vector.tensor_tensor(
+                out=result[:].rearrange("c n j f -> c j n f"),
+                in0=turned[:].rearrange("c j (n f) -> c j n f", n=BATCH),
+                in1=bias_f32[:, b, :].unsqueeze(2).unsqueeze(3).to_broadcast([P, RUN, BATCH, HW]),
+                op=ALU.add,
+            )
+            nc.sync.dma_start(out=out_by_bank[b], in_=result[:].rearrange("c n j f -> c n (j f)"))

@@ -19,6 +19,7 @@ PIXELS = BATCH * HW
 PASSES = CHANNELS // K_PASS
 BANK_COLS = 512
 BANKS = CHANNELS // BANK_COLS
+PARTS = ((0, BANKS - 1), (BANKS - 1, BANKS))
 RUN = BANK_COLS // P
 PLANES_PER_TILE = 4
 QUADRANTS = 4
@@ -55,11 +56,10 @@ def tile_caps_bn_w_e_kernel(tc, x, weight_words, weight_scales, bias, out):
 
         w_sb = keep.tile([P, PASSES, CHANNELS], U32, align_bytes=64)
         w_dram = weight_words.rearrange("g p n t -> p g (n t)").bitcast(I32)
-        for g in range(PASSES - 1):
-            nc.sync.dma_start(out=w_sb[:, g, :].bitcast(I32), in_=w_dram[:, g, :])
-        for b in range(BANKS):
-            cols = slice(b * BANK_COLS, (b + 1) * BANK_COLS)
-            nc.sync.dma_start(out=w_sb[:, PASSES - 1, cols].bitcast(I32), in_=w_dram[:, PASSES - 1, cols])
+        for first_bank, end_bank in PARTS:
+            cols = slice(first_bank * BANK_COLS, end_bank * BANK_COLS)
+            for g in range(PASSES):
+                nc.sync.dma_start(out=w_sb[:, g, cols].bitcast(I32), in_=w_dram[:, g, cols])
 
         bias_bf = keep.tile([P, BANKS, RUN], BF16)
         nc.scalar.dma_start(out=bias_bf[:], in_=bias.rearrange("(b c j) -> c b j", c=P, j=RUN))
@@ -118,23 +118,26 @@ def tile_caps_bn_w_e_kernel(tc, x, weight_words, weight_scales, bias, out):
                 stop=(g == PASSES - 1),
             )
 
-        for g in range(PASSES - 1):
-            for b in range(BANKS):
-                mx_pass(g, b)
-
         out_by_bank = out.rearrange("n (b c j) h w -> b c n (j h w)", c=P, j=RUN)
-        for b in range(BANKS):
-            mx_pass(PASSES - 1, b)
+        result = keep.tile([P, BANKS, BATCH, RUN, HW], F32)
+
+        def finish_bank(b):
             sorted_cols = work.tile([P, RUN, P], F32)
             nc.scalar.copy(out=sorted_cols[:], in_=acc[b][:].rearrange("p (c j) -> p j c", j=RUN))
             turned = psum.tile([P, RUN, PIXELS], F32, tag="bank")
             for j in range(RUN):
                 nc.tensor.transpose(turned[:, j, :], sorted_cols[:, j, :], ident[:])
-            result = work.tile([P, BATCH, RUN, HW], F32)
             nc.vector.tensor_tensor(
-                out=result[:].rearrange("c n j f -> c j n f"),
+                out=result[:, b].rearrange("c n j f -> c j n f"),
                 in0=turned[:].rearrange("c j (n f) -> c j n f", n=BATCH),
                 in1=bias_f32[:, b, :].unsqueeze(2).unsqueeze(3).to_broadcast([P, RUN, BATCH, HW]),
                 op=ALU.add,
             )
-            nc.sync.dma_start(out=out_by_bank[b], in_=result[:].rearrange("c n j f -> c n (j f)"))
+            nc.sync.dma_start(out=out_by_bank[b], in_=result[:, b].rearrange("c n j f -> c n (j f)"))
+
+        for first_bank, end_bank in PARTS:
+            for g in range(PASSES):
+                for b in range(first_bank, end_bank):
+                    mx_pass(g, b)
+            for b in range(first_bank, end_bank):
+                finish_bank(b)

@@ -34,12 +34,7 @@ def tile_caps_bn_w_e_kernel(tc, x, weight_words, weight_scales, bias, out):
         keep = stack.enter_context(tc.tile_pool(name="keep", bufs=1))
         work = stack.enter_context(tc.tile_pool(name="work", bufs=3))
         psum = stack.enter_context(tc.psum_pool(name="psum", bufs=BANKS))
-
-        x_sb = keep.tile([P, BATCH, PASSES, PACK, HW], BF16)
-        nc.sync.dma_start(
-            out=x_sb[:].rearrange("p n g t f -> p n g (t f)"),
-            in_=x.rearrange("n (g p t) h w -> p n g (t h w)", p=P, t=PACK),
-        )
+        stack.enter_context(tc.manual_schedule())
 
         planes = [
             keep.tile([P, CHANNELS], U8, align_bytes=64, name="planes%d" % a) for a in range(PASSES // PLANES_PER_TILE)
@@ -54,6 +49,16 @@ def tile_caps_bn_w_e_kernel(tc, x, weight_words, weight_scales, bias, out):
                     in_=scales_i32[PLANES_PER_TILE * a : PLANES_PER_TILE * (a + 1), 4 * quad : 4 * quad + 4, :],
                 )
 
+        x_sb = keep.tile([P, BATCH, PASSES, PACK, HW], BF16)
+        nc.sync.dma_start(
+            out=x_sb[:].rearrange("p n g t f -> p n g (t f)"),
+            in_=x.rearrange("n (g p t) h w -> p n g (t h w)", p=P, t=PACK),
+        )
+
+        bias_rows = keep.tile([P, BANK_COLS], BF16)
+        nc.vector.memset(bias_rows[:], 0.0)
+        nc.scalar.dma_start(out=bias_rows[0:BANKS, :], in_=bias.rearrange("(b i) -> b i", i=BANK_COLS))
+
         w_sb = keep.tile([P, PASSES, CHANNELS], U32, align_bytes=64)
         w_dram = weight_words.rearrange("g p n t -> p g (n t)").bitcast(I32)
         for first_bank, end_bank in PARTS:
@@ -61,13 +66,16 @@ def tile_caps_bn_w_e_kernel(tc, x, weight_words, weight_scales, bias, out):
             for g in range(PASSES):
                 nc.sync.dma_start(out=w_sb[:, g, cols].bitcast(I32), in_=w_dram[:, g, cols])
 
-        bias_bf = keep.tile([P, BANKS, RUN], BF16)
-        nc.scalar.dma_start(out=bias_bf[:], in_=bias.rearrange("(b c j) -> c b j", c=P, j=RUN))
-        bias_f32 = keep.tile([P, BANKS, RUN], F32)
-        nc.vector.tensor_copy(out=bias_f32[:], in_=bias_bf[:])
-
         ident = keep.tile([P, P], F32)
         make_identity(nc, ident[:])
+
+        bias_sorted = keep.tile([P, RUN, P], F32)
+        nc.vector.tensor_copy(out=bias_sorted[:], in_=bias_rows[:].rearrange("b (c j) -> b j c", j=RUN))
+        bias_turned = psum.tile([P, RUN, P], F32, tag="bank")
+        for j in range(RUN):
+            nc.tensor.transpose(bias_turned[:, j, :], bias_sorted[:, j, :], ident[:])
+        bias_f32 = keep.tile([P, BANKS, RUN], F32)
+        nc.vector.tensor_copy(out=bias_f32[:].rearrange("c b j -> c j b"), in_=bias_turned[:, :, 0:BANKS])
 
         stats = keep.tile([P, PASSES, PACK, BN_STATS_DIM], F32)
         mean_var = keep.tile([P, PASSES, PACK, 2], F32)

@@ -19,7 +19,7 @@ PIXELS = BATCH * HW
 PASSES = CHANNELS // K_PASS
 BANK_COLS = 512
 BANKS = CHANNELS // BANK_COLS
-PARTS = ((0, BANKS - 1), (BANKS - 1, BANKS))
+PARTS = ((0, 5), (5, 7), (7, 8))
 RUN = BANK_COLS // P
 PLANES_PER_TILE = 4
 QUADRANTS = 4

@@ -36,6 +36,12 @@ def tile_caps_bn_w_e_kernel(tc, x, weight_words, weight_scales, bias, out):
         psum = stack.enter_context(tc.psum_pool(name="psum", bufs=BANKS))
         stack.enter_context(tc.manual_schedule())
 
+        x_sb = keep.tile([P, BATCH, PASSES, PACK, HW], BF16)
+        nc.sync.dma_start(
+            out=x_sb[:].rearrange("p n g t f -> p n g (t f)"),
+            in_=x.rearrange("n (g p t) h w -> p n g (t h w)", p=P, t=PACK),
+        )
+
         planes = [
             keep.tile([P, CHANNELS], U8, align_bytes=64, name="planes%d" % a) for a in range(PASSES // PLANES_PER_TILE)
         ]
@@ -48,12 +54,6 @@ def tile_caps_bn_w_e_kernel(tc, x, weight_words, weight_scales, bias, out):
                     out=plane_tile[32 * quad : 32 * quad + 4 * PLANES_PER_TILE, :].bitcast(I32),
                     in_=scales_i32[PLANES_PER_TILE * a : PLANES_PER_TILE * (a + 1), 4 * quad : 4 * quad + 4, :],
                 )
-
-        x_sb = keep.tile([P, BATCH, PASSES, PACK, HW], BF16)
-        nc.sync.dma_start(
-            out=x_sb[:].rearrange("p n g t f -> p n g (t f)"),
-            in_=x.rearrange("n (g p t) h w -> p n g (t h w)", p=P, t=PACK),
-        )
 
         bias_rows = keep.tile([P, BANK_COLS], BF16)
         nc.vector.memset(bias_rows[:], 0.0)

@@ -10,6 +10,7 @@ I32 = mybir.dt.int32
 U32 = mybir.dt.uint32
 U8 = mybir.dt.uint8
 ALU = mybir.AluOpType
+ACT = mybir.ActivationFunctionType
 
 P = 128
 PACK = 4
@@ -20,6 +21,7 @@ PASSES = CHANNELS // K_PASS
 BANK_COLS = 512
 BANKS = CHANNELS // BANK_COLS
 PARTS = ((0, 5), (5, 7), (7, 8))
+LAST_BANK = BANKS - 1
 RUN = BANK_COLS // P
 PLANES_PER_TILE = 4
 QUADRANTS = 4
@@ -69,19 +71,23 @@ def tile_caps_bn_w_e_kernel(tc, x, weight_words, weight_scales, bias, out):
         ident = keep.tile([P, P], F32)
         make_identity(nc, ident[:])
 
-        bias_sorted = keep.tile([P, RUN, P], F32)
-        nc.vector.tensor_copy(out=bias_sorted[:], in_=bias_rows[:].rearrange("b (c j) -> b j c", j=RUN))
-        bias_turned = psum.tile([P, RUN, P], F32, tag="bank")
-        for j in range(RUN):
-            nc.tensor.transpose(bias_turned[:, j, :], bias_sorted[:, j, :], ident[:])
-        bias_f32 = keep.tile([P, BANKS, RUN], F32)
-        nc.vector.tensor_copy(out=bias_f32[:].rearrange("c b j -> c j b"), in_=bias_turned[:, :, 0:BANKS])
-
         stats = keep.tile([P, PASSES, PACK, BN_STATS_DIM], F32)
         mean_var = keep.tile([P, PASSES, PACK, 2], F32)
         for g in range(PASSES):
             for t in range(PACK):
                 nc.vector.bn_stats(out=stats[:, g, t, :], in_=x_sb[:, :, g, t, :])
+
+        bias_sorted = keep.tile([P, RUN, P], F32)
+        nc.vector.tensor_copy(out=bias_sorted[:], in_=bias_rows[:].rearrange("b (c j) -> b j c", j=RUN))
+        bias_turned = psum.tile([P, RUN, P], F32, tag="bank")
+        for j in range(RUN):
+            nc.tensor.transpose(bias_turned[:, j, :], bias_sorted[:, j, :], ident[:])
+        bias_plain = keep.tile([P, RUN, P], F32)
+        nc.vector.tensor_copy(out=bias_plain[:], in_=bias_rows[:].rearrange("b (i m) -> b i m", i=RUN))
+        bias_plain_turned = psum.tile([P, RUN, P], F32, tag="bank")
+        for i in range(RUN):
+            nc.tensor.transpose(bias_plain_turned[:, i, :], bias_plain[:, i, :], ident[:])
+
         for g in range(PASSES):
             for t in range(PACK):
                 nc.vector.bn_aggr(out=mean_var[:, g, t, :], in_=stats[:, g, t, :])
@@ -111,7 +117,12 @@ def tile_caps_bn_w_e_kernel(tc, x, weight_words, weight_scales, bias, out):
                 in_=grouped[:, g, :, :].rearrange("p c t -> p (c t)"),
             )
 
-        acc = [psum.tile([P, BANK_COLS], F32, name="acc%d" % b, tag="bank") for b in range(BANKS)]
+        bias_f32 = keep.tile([P, BANKS, RUN], F32)
+        nc.vector.tensor_copy(out=bias_f32[:].rearrange("c b j -> c j b"), in_=bias_turned[:, :, 0:BANKS])
+        bias_last = keep.tile([P, RUN], F32)
+        nc.vector.tensor_copy(out=bias_last[:], in_=bias_plain_turned[:, :, LAST_BANK])
+
+        acc = [psum.tile([P, BANK_COLS], F32, name="acc%d" % b, tag="bank") for b in range(LAST_BANK)]
 
         def mx_pass(g, b):
             cols = slice(b * BANK_COLS, (b + 1) * BANK_COLS)
@@ -127,7 +138,7 @@ def tile_caps_bn_w_e_kernel(tc, x, weight_words, weight_scales, bias, out):
             )
 
         out_by_bank = out.rearrange("n (b c j) h w -> b c n (j h w)", c=P, j=RUN)
-        result = keep.tile([P, BANKS, BATCH, RUN, HW], F32)
+        result = keep.tile([P, LAST_BANK, BATCH, RUN, HW], F32)
 
         def finish_bank(b):
             sorted_cols = work.tile([P, RUN, P], F32)
@@ -143,9 +154,39 @@ def tile_caps_bn_w_e_kernel(tc, x, weight_words, weight_scales, bias, out):
             )
             nc.sync.dma_start(out=out_by_bank[b], in_=result[:, b].rearrange("c n j f -> c n (j f)"))
 
-        for first_bank, end_bank in PARTS:
+        for first_bank, end_bank in PARTS[:-1]:
             for g in range(PASSES):
                 for b in range(first_bank, end_bank):
                     mx_pass(g, b)
             for b in range(first_bank, end_bank):
                 finish_bank(b)
+
+        acc_last = [psum.tile([P, PIXELS], F32, name="acc_last%d" % i, tag="bank") for i in range(RUN)]
+        for g in range(PASSES):
+            first_row = 4 * (g % PLANES_PER_TILE)
+            for i in range(RUN):
+                cols = slice(LAST_BANK * BANK_COLS + i * P, LAST_BANK * BANK_COLS + (i + 1) * P)
+                nc.tensor.matmul_mx(
+                    out=acc_last[i][:],
+                    lhsT=w_sb[:, g, cols].bitcast(FP8X4),
+                    lhsT_scale=planes[g // PLANES_PER_TILE][first_row:P, cols],
+                    rhs=xq_words[:, g, :].bitcast(FP8X4),
+                    rhs_scale=xq_scales[:, g, :],
+                    start=(g == 0),
+                    stop=(g == PASSES - 1),
+                )
+        out_last = out.rearrange("n (b i m) h w -> b i m n (h w)", i=RUN, m=P)[LAST_BANK]
+        result_last = keep.tile([P, RUN, BATCH, HW], F32)
+        for i in range(RUN):
+            if i % 2 == 0:
+                nc.scalar.activation(
+                    out=result_last[:, i].rearrange("m n f -> m (n f)"),
+                    in_=acc_last[i][:],
+                    func=ACT.Identity,
+                    bias=bias_last[:, i : i + 1],
+                )
+            else:
+                nc.vector.tensor_scalar_add(
+                    out=result_last[:, i].rearrange("m n f -> m (n f)"), in0=acc_last[i][:], scalar1=bias_last[:, i : i + 1]
+                )
+            nc.sync.dma_start(out=out_last[i], in_=result_last[:, i])

@@ -50,8 +50,8 @@ def tile_caps_bn_w_e_kernel(tc, x, weight_words, weight_scales, bias, out):
         scales_i32 = weight_scales.bitcast(I32)
         for plane_tile in planes:
             nc.vector.memset(plane_tile[:].bitcast(I32), 0)
-        for a, plane_tile in enumerate(planes):
-            for quad in range(QUADRANTS):
+        for quad in (2, 3, 0, 1):
+            for a, plane_tile in enumerate(planes):
                 nc.sync.dma_start(
                     out=plane_tile[32 * quad : 32 * quad + 4 * PLANES_PER_TILE, :].bitcast(I32),
                     in_=scales_i32[PLANES_PER_TILE * a : PLANES_PER_TILE * (a + 1), 4 * quad : 4 * quad + 4, :],

@@ -50,7 +50,7 @@ def tile_caps_bn_w_e_kernel(tc, x, weight_words, weight_scales, bias, out):
         scales_i32 = weight_scales.bitcast(I32)
         for plane_tile in planes:
             nc.vector.memset(plane_tile[:].bitcast(I32), 0)
-        for quad in (2, 3, 0, 1):
+        for quad in (2, 3, 1, 0):
             for a, plane_tile in enumerate(planes):
                 nc.sync.dma_start(
                     out=plane_tile[32 * quad : 32 * quad + 4 * PLANES_PER_TILE, :].bitcast(I32),

from contextlib import ExitStack

import concourse.mybir as mybir
from concourse.masks import make_identity

FP8X4 = mybir.dt.float8_e4m3fn_x4
BF16 = mybir.dt.bfloat16
F32 = mybir.dt.float32
I32 = mybir.dt.int32
U32 = mybir.dt.uint32
U8 = mybir.dt.uint8
ALU = mybir.AluOpType
ACT = mybir.ActivationFunctionType

P = 128
PACK = 4
K_PASS = P * PACK
BATCH, CHANNELS, HW = 2, 4096, 64
PIXELS = BATCH * HW
PASSES = CHANNELS // K_PASS
BANK_COLS = 512
BANKS = CHANNELS // BANK_COLS
PARTS = ((0, 5), (5, 7), (7, 8))
LAST_BANK = BANKS - 1
RUN = BANK_COLS // P
PLANES_PER_TILE = 4
QUADRANTS = 4
EPS = 1e-5
BN_STATS_DIM = 6
FLOPS = 2 * CHANNELS * CHANNELS * PIXELS


def tile_caps_bn_w_e_kernel(tc, x, weight_words, weight_scales, bias, out):
    nc = tc.nc
    with ExitStack() as stack:
        keep = stack.enter_context(tc.tile_pool(name="keep", bufs=1))
        work = stack.enter_context(tc.tile_pool(name="work", bufs=3))
        psum = stack.enter_context(tc.psum_pool(name="psum", bufs=BANKS))
        stack.enter_context(tc.manual_schedule())

        x_sb = keep.tile([P, BATCH, PASSES, PACK, HW], BF16)
        nc.sync.dma_start(
            out=x_sb[:].rearrange("p n g t f -> p n g (t f)"),
            in_=x.rearrange("n (g p t) h w -> p n g (t h w)", p=P, t=PACK),
        )

        planes = [
            keep.tile([P, CHANNELS], U8, align_bytes=64, name="planes%d" % a) for a in range(PASSES // PLANES_PER_TILE)
        ]
        scales_i32 = weight_scales.bitcast(I32)
        for plane_tile in planes:
            nc.vector.memset(plane_tile[:].bitcast(I32), 0)
        for quad in (2, 3, 1, 0):
            for a, plane_tile in enumerate(planes):
                nc.sync.dma_start(
                    out=plane_tile[32 * quad : 32 * quad + 4 * PLANES_PER_TILE, :].bitcast(I32),
                    in_=scales_i32[PLANES_PER_TILE * a : PLANES_PER_TILE * (a + 1), 4 * quad : 4 * quad + 4, :],
                )

        bias_rows = keep.tile([P, BANK_COLS], BF16)
        nc.vector.memset(bias_rows[:], 0.0)
        nc.scalar.dma_start(out=bias_rows[0:BANKS, :], in_=bias.rearrange("(b i) -> b i", i=BANK_COLS))

        w_sb = keep.tile([P, PASSES, CHANNELS], U32, align_bytes=64)
        w_dram = weight_words.rearrange("g p n t -> p g (n t)").bitcast(I32)
        for first_bank, end_bank in PARTS:
            cols = slice(first_bank * BANK_COLS, end_bank * BANK_COLS)
            for g in range(PASSES):
                nc.sync.dma_start(out=w_sb[:, g, cols].bitcast(I32), in_=w_dram[:, g, cols])

        ident = keep.tile([P, P], F32)
        make_identity(nc, ident[:])

        stats = keep.tile([P, PASSES, PACK, BN_STATS_DIM], F32)
        mean_var = keep.tile([P, PASSES, PACK, 2], F32)
        for g in range(PASSES):
            for t in range(PACK):
                nc.vector.bn_stats(out=stats[:, g, t, :], in_=x_sb[:, :, g, t, :])

        bias_sorted = keep.tile([P, RUN, P], F32)
        nc.vector.tensor_copy(out=bias_sorted[:], in_=bias_rows[:].rearrange("b (c j) -> b j c", j=RUN))
        bias_turned = psum.tile([P, RUN, P], F32, tag="bank")
        for j in range(RUN):
            nc.tensor.transpose(bias_turned[:, j, :], bias_sorted[:, j, :], ident[:])
        bias_plain = keep.tile([P, RUN, P], F32)
        nc.vector.tensor_copy(out=bias_plain[:], in_=bias_rows[:].rearrange("b (i m) -> b i m", i=RUN))
        bias_plain_turned = psum.tile([P, RUN, P], F32, tag="bank")
        for i in range(RUN):
            nc.tensor.transpose(bias_plain_turned[:, i, :], bias_plain[:, i, :], ident[:])

        for g in range(PASSES):
            for t in range(PACK):
                nc.vector.bn_aggr(out=mean_var[:, g, t, :], in_=stats[:, g, t, :])
        var_eps = keep.tile([P, PASSES, PACK], F32)
        nc.vector.tensor_scalar_add(out=var_eps[:], in0=mean_var[:, :, :, 1], scalar1=EPS)
        std = keep.tile([P, PASSES, PACK], F32)
        nc.scalar.sqrt(out=std[:], in_=var_eps[:])
        rstd = keep.tile([P, PASSES, PACK], F32)
        nc.vector.reciprocal(out=rstd[:], in_=std[:])

        grouped = keep.tile([P, PASSES, PIXELS, PACK], BF16, align_bytes=64)
        xq_words = keep.tile([P, PASSES, PIXELS], U32, align_bytes=64)
        xq_scales = keep.tile([P, PASSES, PIXELS], U8, align_bytes=64)
        for g in range(PASSES):
            for t in range(PACK):
                nc.vector.tensor_scalar(
                    out=grouped[:, g, :, t].rearrange("p (n f) -> p n f", n=BATCH),
                    in0=x_sb[:, :, g, t, :],
                    scalar1=mean_var[:, g, t, 0:1],
                    scalar2=rstd[:, g, t : t + 1],
                    op0=ALU.subtract,
                    op1=ALU.mult,
                )
            nc.vector.quantize_mx(
                out=xq_words[:, g, :].bitcast(FP8X4),
                scales=xq_scales[:, g, :],
                in_=grouped[:, g, :, :].rearrange("p c t -> p (c t)"),
            )

        bias_f32 = keep.tile([P, BANKS, RUN], F32)
        nc.vector.tensor_copy(out=bias_f32[:].rearrange("c b j -> c j b"), in_=bias_turned[:, :, 0:BANKS])
        bias_last = keep.tile([P, RUN], F32)
        nc.vector.tensor_copy(out=bias_last[:], in_=bias_plain_turned[:, :, LAST_BANK])

        acc = [psum.tile([P, BANK_COLS], F32, name="acc%d" % b, tag="bank") for b in range(LAST_BANK)]

        def mx_pass(g, b):
            cols = slice(b * BANK_COLS, (b + 1) * BANK_COLS)
            first_row = 4 * (g % PLANES_PER_TILE)
            nc.tensor.matmul_mx(
                out=acc[b][:],
                lhsT=xq_words[:, g, :].bitcast(FP8X4),
                lhsT_scale=xq_scales[:, g, :],
                rhs=w_sb[:, g, cols].bitcast(FP8X4),
                rhs_scale=planes[g // PLANES_PER_TILE][first_row:P, cols],
                start=(g == 0),
                stop=(g == PASSES - 1),
            )

        out_by_bank = out.rearrange("n (b c j) h w -> b c n (j h w)", c=P, j=RUN)
        result = keep.tile([P, LAST_BANK, BATCH, RUN, HW], F32)

        def finish_bank(b):
            sorted_cols = work.tile([P, RUN, P], F32)
            nc.scalar.copy(out=sorted_cols[:], in_=acc[b][:].rearrange("p (c j) -> p j c", j=RUN))
            turned = psum.tile([P, RUN, PIXELS], F32, tag="bank")
            for j in range(RUN):
                nc.tensor.transpose(turned[:, j, :], sorted_cols[:, j, :], ident[:])
            nc.vector.tensor_tensor(
                out=result[:, b].rearrange("c n j f -> c j n f"),
                in0=turned[:].rearrange("c j (n f) -> c j n f", n=BATCH),
                in1=bias_f32[:, b, :].unsqueeze(2).unsqueeze(3).to_broadcast([P, RUN, BATCH, HW]),
                op=ALU.add,
            )
            nc.sync.dma_start(out=out_by_bank[b], in_=result[:, b].rearrange("c n j f -> c n (j f)"))

        for first_bank, end_bank in PARTS[:-1]:
            for g in range(PASSES):
                for b in range(first_bank, end_bank):
                    mx_pass(g, b)
            for b in range(first_bank, end_bank):
                finish_bank(b)

        acc_last = [psum.tile([P, PIXELS], F32, name="acc_last%d" % i, tag="bank") for i in range(RUN)]
        for g in range(PASSES):
            first_row = 4 * (g % PLANES_PER_TILE)
            for i in range(RUN):
                cols = slice(LAST_BANK * BANK_COLS + i * P, LAST_BANK * BANK_COLS + (i + 1) * P)
                nc.tensor.matmul_mx(
                    out=acc_last[i][:],
                    lhsT=w_sb[:, g, cols].bitcast(FP8X4),
                    lhsT_scale=planes[g // PLANES_PER_TILE][first_row:P, cols],
                    rhs=xq_words[:, g, :].bitcast(FP8X4),
                    rhs_scale=xq_scales[:, g, :],
                    start=(g == 0),
                    stop=(g == PASSES - 1),
                )
        out_last = out.rearrange("n (b i m) h w -> b i m n (h w)", i=RUN, m=P)[LAST_BANK]
        result_last = keep.tile([P, RUN, BATCH, HW], F32)
        for i in range(RUN):
            if i % 2 == 0:
                nc.scalar.activation(
                    out=result_last[:, i].rearrange("m n f -> m (n f)"),
                    in_=acc_last[i][:],
                    func=ACT.Identity,
                    bias=bias_last[:, i : i + 1],
                )
            else:
                nc.vector.tensor_scalar_add(
                    out=result_last[:, i].rearrange("m n f -> m (n f)"), in0=acc_last[i][:], scalar1=bias_last[:, i : i + 1]
                )
            nc.sync.dma_start(out=out_last[i], in_=result_last[:, i])
